import numpy as np
import ml_dtypes


def mxq(x, axis, fmt="e4m3"):
    dtype, down = {"e4m3": (ml_dtypes.float8_e4m3fn, 7), "e5m2": (ml_dtypes.float8_e5m2, 14)}[fmt]
    v = np.moveaxis(np.asarray(x, np.float32).astype(ml_dtypes.bfloat16).astype(np.float64), axis, -1)
    blocks = v.reshape(v.shape[:-1] + (-1, 32))
    amax = np.abs(blocks).max(-1, keepdims=True)
    byte = np.maximum(np.where(amax > 0, np.frexp(amax)[1] - 1 + 127, 0) - down, 1)
    scale = np.exp2(byte - 127.0)
    codes = (blocks / scale).astype(np.float32).astype(dtype).astype(np.float64)
    return np.moveaxis((codes * scale).reshape(v.shape), -1, axis)


WIDE = False


def mx_kscale(k):
    if not WIDE:
        return np.ones(k)
    levels = np.array([20, -20, 10, -10, 0])
    a = np.random.permutation(np.resize(levels, k // 512 * 4)).reshape(k // 512, 4)
    idx = np.arange(k)
    return np.exp2(a[idx // 512, idx % 128 // 32])


BF16 = ml_dtypes.bfloat16


def bf(x):
    return np.asarray(x, np.float32).astype(BF16)


def f64(x):
    return np.asarray(x).astype(np.float64)


B, L, C, K, D_MODEL, H, D_LLM = 2, 256, 16, 100, 512, 32, 512
D_KEYS = D_MODEL // H
G = H * D_KEYS
T = B * L


def setup_inputs():
    s = mx_kscale(T).reshape(B, L)
    attn_ctx = np.random.standard_normal((B, C, L, H, D_KEYS)) * 0.5 * s[:, None, :, None, None]
    Wo = np.random.standard_normal((C, H, D_KEYS, D_LLM)) * 2.0 / np.sqrt(G)
    bo = np.random.standard_normal((C, D_LLM)) * 0.5
    cluster_probs = np.random.uniform(size=(B, L, C))
    g = np.random.standard_normal((B, L, D_LLM)) * np.exp2(np.random.randint(-12, 1, (B, L, 1))) / s[:, :, None]
    return {
        "attn_ctx": bf(attn_ctx),
        "Wo": bf(Wo),
        "bo": bf(bo),
        "cluster_probs": bf(cluster_probs),
        "grad_out": bf(g),
    }


def reference(attn_ctx, Wo, bo, cluster_probs, grad_out):
    o = f64(attn_ctx).reshape(B, C, L, G).transpose(1, 0, 2, 3).reshape(C, T, G)
    p = f64(cluster_probs).reshape(T, C)
    g = f64(grad_out).reshape(T, D_LLM)
    gp = p.T[:, :, None] * g[None, :, :]
    dw = mxq(o, 1, "e4m3").transpose(0, 2, 1) @ mxq(gp, 1, "e5m2")
    return dw.reshape(C, H, D_KEYS, D_LLM)

@@ -1,0 +1,117 @@
+import concourse.mybir as mybir
+
+F32 = mybir.dt.float32
+BF16 = mybir.dt.bfloat16
+U32 = mybir.dt.uint32
+U8 = mybir.dt.uint8
+E4M3_X4 = mybir.dt.float8_e4m3fn_x4
+E5M2_X4 = mybir.dt.float8_e5m2_x4
+
+P = 128
+PACK = 4
+BATCH = 2
+PAIR = 2
+CLUSTERS = 16
+G = 512
+E = 512
+M_TILE = 128
+M_TILES = G // M_TILE
+
+RUN = 4
+RUNS = G // RUN
+VECTOR_RUNS = RUNS * 5 // 8
+
+FLOPS = 2 * CLUSTERS * G * E * P * PACK
+BYTES = 2 * CLUSTERS * G * P * PACK + 2 * CLUSTERS * P * PACK + 2 * E * P * PACK + 4 * CLUSTERS * G * E
+
+
+def regroup(nc, grouped, rows):
+    dst = grouped.rearrange("p (r i) t -> p r t i", i=RUN)
+    src = rows.rearrange("p t (r i) -> p r t i", i=RUN)
+    nc.vector.tensor_copy(out=dst[:, :VECTOR_RUNS], in_=src[:, :VECTOR_RUNS])
+    nc.scalar.copy(out=dst[:, VECTOR_RUNS:], in_=src[:, VECTOR_RUNS:])
+
+
+def tile_model_pa_kernel(tc, attn_ctx, Wo, bo, cluster_probs, grad_out, out):
+    nc = tc.nc
+
+    attn_view = attn_ctx.rearrange("b c (p e) h d -> p b c (e h d)", e=PAIR)
+    probs_view = cluster_probs.rearrange("b (p e) c -> p b (e c)", e=PAIR)
+    grad_view = grad_out.rearrange("b (p e) n -> p b (e n)", e=PAIR)
+    out_view = out.rearrange("c h d e -> c (h d) e").rearrange("c (i m) e -> c m i e", m=M_TILE)
+
+    with tc.tile_pool(name="const", bufs=1) as const, tc.tile_pool(
+        name="rows", bufs=CLUSTERS
+    ) as rows_pool, tc.tile_pool(name="work", bufs=3) as work, tc.tile_pool(
+        name="result", bufs=4
+    ) as result_pool, tc.psum_pool(name="psum", bufs=8) as psum:
+        probs_rows = const.tile([P, PACK, CLUSTERS], BF16)
+        nc.sync.dma_start(
+            out=probs_rows[:].rearrange("p (b e) c -> p b (e c)", b=BATCH), in_=probs_view
+        )
+        grad_rows = const.tile([P, PACK, E], BF16)
+        nc.sync.dma_start(
+            out=grad_rows[:].rearrange("p (b e) n -> p b (e n)", b=BATCH), in_=grad_view
+        )
+        attn_rows = []
+        for c in range(CLUSTERS):
+            rows = rows_pool.tile([P, PACK, G], BF16, name="rows")
+            nc.sync.dma_start(
+                out=rows[:].rearrange("p (b e) g -> p b (e g)", b=BATCH), in_=attn_view[:, :, c, :]
+            )
+            attn_rows.append(rows)
+
+        probs = const.tile([P, CLUSTERS, PACK], BF16)
+        nc.vector.tensor_copy(out=probs[:], in_=probs_rows[:].rearrange("p t c -> p c t"))
+        grad = const.tile([P, E, PACK], BF16)
+        regroup(nc, grad[:], grad_rows[:])
+
+        def quantise_cluster(c):
+            attn = work.tile([P, G, PACK], BF16, align_bytes=64)
+            regroup(nc, attn[:], attn_rows[c][:])
+            gp = work.tile([P, E, PACK], BF16, align_bytes=64)
+            nc.vector.tensor_tensor(
+                out=gp[:],
+                in0=grad[:],
+                in1=probs[:, c, :].unsqueeze(1).to_broadcast([P, E, PACK]),
+                op=mybir.AluOpType.mult,
+            )
+            attn_codes = work.tile([P, G], U32, align_bytes=64)
+            attn_scales = work.tile([P, G], U8, align_bytes=64)
+            nc.vector.quantize_mx(
+                out=attn_codes[:].bitcast(E4M3_X4),
+                scales=attn_scales[:],
+                in_=attn[:].rearrange("p w t -> p (w t)"),
+            )
+            gp_codes = work.tile([P, E], U32, align_bytes=64)
+            gp_scales = work.tile([P, E], U8, align_bytes=64)
+            nc.vector.quantize_mx(
+                out=gp_codes[:].bitcast(E5M2_X4),
+                scales=gp_scales[:],
+                in_=gp[:].rearrange("p w t -> p (w t)"),
+            )
+            return attn_codes, attn_scales, gp_codes, gp_scales
+
+        def multiply_cluster(c, operands):
+            attn_codes, attn_scales, gp_codes, gp_scales = operands
+            result = result_pool.tile([P, M_TILES, E], F32)
+            for i in range(M_TILES):
+                m_cols = slice(i * M_TILE, (i + 1) * M_TILE)
+                acc = psum.tile([M_TILE, E], F32)
+                nc.tensor.matmul_mx(
+                    out=acc[:],
+                    lhsT=attn_codes[:, m_cols].bitcast(E4M3_X4),
+                    lhsT_scale=attn_scales[:, m_cols],
+                    rhs=gp_codes[:].bitcast(E5M2_X4),
+                    rhs_scale=gp_scales[:],
+                    start=True,
+                    stop=True,
+                )
+                nc.scalar.copy(out=result[:, i, :], in_=acc[:])
+            nc.sync.dma_start(out=out_view[c], in_=result[:])
+
+        operands = quantise_cluster(0)
+        for c in range(CLUSTERS):
+            following = quantise_cluster(c + 1) if c + 1 < CLUSTERS else None
+            multiply_cluster(c, operands)
+            operands = following

@@ -20,16 +20,15 @@ M_TILES = G // M_TILE
 RUN = 4
 RUNS = G // RUN
 VECTOR_RUNS = RUNS * 5 // 8
+assert RUN == M_TILES
 
 FLOPS = 2 * CLUSTERS * G * E * P * PACK
 BYTES = 2 * CLUSTERS * G * P * PACK + 2 * CLUSTERS * P * PACK + 2 * E * P * PACK + 4 * CLUSTERS * G * E
 
 
 def regroup(nc, grouped, rows):
-    dst = grouped.rearrange("p (r i) t -> p r t i", i=RUN)
-    src = rows.rearrange("p t (r i) -> p r t i", i=RUN)
-    nc.vector.tensor_copy(out=dst[:, :VECTOR_RUNS], in_=src[:, :VECTOR_RUNS])
-    nc.scalar.copy(out=dst[:, VECTOR_RUNS:], in_=src[:, VECTOR_RUNS:])
+    nc.vector.tensor_copy(out=grouped[:, :VECTOR_RUNS], in_=rows[:, :VECTOR_RUNS])
+    nc.scalar.copy(out=grouped[:, VECTOR_RUNS:], in_=rows[:, VECTOR_RUNS:])
 
 
 def tile_model_pa_kernel(tc, attn_ctx, Wo, bo, cluster_probs, grad_out, out):
@@ -38,7 +37,7 @@ def tile_model_pa_kernel(tc, attn_ctx, Wo, bo, cluster_probs, grad_out, out):
     attn_view = attn_ctx.rearrange("b c (p e) h d -> p b c (e h d)", e=PAIR)
     probs_view = cluster_probs.rearrange("b (p e) c -> p b (e c)", e=PAIR)
     grad_view = grad_out.rearrange("b (p e) n -> p b (e n)", e=PAIR)
-    out_view = out.rearrange("c h d e -> c (h d) e").rearrange("c (i m) e -> c m i e", m=M_TILE)
+    out_view = out.rearrange("c h d e -> c (h d) e").rearrange("c (m i) e -> c m (i e)", i=M_TILES)
 
     with tc.tile_pool(name="const", bufs=1) as const, tc.tile_pool(
         name="rows", bufs=CLUSTERS
@@ -64,11 +63,19 @@ def tile_model_pa_kernel(tc, attn_ctx, Wo, bo, cluster_probs, grad_out, out):
         probs = const.tile([P, CLUSTERS, PACK], BF16)
         nc.vector.tensor_copy(out=probs[:], in_=probs_rows[:].rearrange("p t c -> p c t"))
         grad = const.tile([P, E, PACK], BF16)
-        regroup(nc, grad[:], grad_rows[:])
+        regroup(
+            nc,
+            grad[:].rearrange("p (r i) t -> p r t i", i=RUN),
+            grad_rows[:].rearrange("p t (r i) -> p r t i", i=RUN),
+        )
 
         def quantise_cluster(c):
             attn = work.tile([P, G, PACK], BF16, align_bytes=64)
-            regroup(nc, attn[:], attn_rows[c][:])
+            regroup(
+                nc,
+                attn[:].rearrange("p (i m) t -> p m t i", i=M_TILES),
+                attn_rows[c][:].rearrange("p t (m i) -> p m t i", i=M_TILES),
+            )
             gp = work.tile([P, E, PACK], BF16, align_bytes=64)
             nc.vector.tensor_tensor(
                 out=gp[:],
@@ -108,7 +115,7 @@ def tile_model_pa_kernel(tc, attn_ctx, Wo, bo, cluster_probs, grad_out, out):
                     stop=True,
                 )
                 nc.scalar.copy(out=result[:, i, :], in_=acc[:])
-            nc.sync.dma_start(out=out_view[c], in_=result[:])
+            nc.sync.dma_start(out=out_view[c], in_=result[:].rearrange("p i e -> p (i e)"))
 
         operands = quantise_cluster(0)
         for c in range(CLUSTERS):

@@ -10,7 +10,6 @@ E5M2_X4 = mybir.dt.float8_e5m2_x4
 P = 128
 PACK = 4
 BATCH = 2
-PAIR = 2
 CLUSTERS = 16
 G = 512
 E = 512
@@ -21,6 +20,8 @@ RUN = 4
 RUNS = G // RUN
 VECTOR_RUNS = RUNS * 5 // 8
 assert RUN == M_TILES
+
+AHEAD = 2
 
 FLOPS = 2 * CLUSTERS * G * E * P * PACK
 BYTES = 2 * CLUSTERS * G * P * PACK + 2 * CLUSTERS * P * PACK + 2 * E * P * PACK + 4 * CLUSTERS * G * E
@@ -34,39 +35,36 @@ def regroup(nc, grouped, rows):
 def tile_model_pa_kernel(tc, attn_ctx, Wo, bo, cluster_probs, grad_out, out):
     nc = tc.nc
 
-    attn_view = attn_ctx.rearrange("b c (p e) h d -> p b c (e h d)", e=PAIR)
-    probs_view = cluster_probs.rearrange("b (p e) c -> p b (e c)", e=PAIR)
-    grad_view = grad_out.rearrange("b (p e) n -> p b (e n)", e=PAIR)
-    out_view = out.rearrange("c h d e -> c (h d) e").rearrange("c (m i) e -> c m (i e)", i=M_TILES)
+    attn_view = attn_ctx.rearrange("b c (q t) h d -> b c q (t h d)", t=PACK)
+    probs_view = cluster_probs.rearrange("b (q t) c -> b q (t c)", t=PACK)
+    grad_view = grad_out.rearrange("b (q t) n -> b q (t n)", t=PACK)
+    out_view = out.rearrange("c h d e -> c (h d) e").rearrange("c (m i) e -> c m i e", i=M_TILES)
 
     with tc.tile_pool(name="const", bufs=1) as const, tc.tile_pool(
         name="rows", bufs=CLUSTERS
-    ) as rows_pool, tc.tile_pool(name="work", bufs=3) as work, tc.tile_pool(
-        name="result", bufs=4
-    ) as result_pool, tc.psum_pool(name="psum", bufs=8) as psum:
+    ) as rows_pool, tc.tile_pool(name="work", bufs=AHEAD + 2) as work, tc.tile_pool(
+        name="result", bufs=8
+    ) as result_pool, tc.psum_pool(name="psum", bufs=8) as psum, tc.manual_schedule():
+        def load_tokens(rows, view):
+            for b in range(BATCH):
+                nc.sync.dma_start(out=rows[b:P:BATCH].rearrange("p t w -> p (t w)"), in_=view[b])
+
         probs_rows = const.tile([P, PACK, CLUSTERS], BF16)
-        nc.sync.dma_start(
-            out=probs_rows[:].rearrange("p (b e) c -> p b (e c)", b=BATCH), in_=probs_view
-        )
+        load_tokens(probs_rows, probs_view)
         grad_rows = const.tile([P, PACK, E], BF16)
-        nc.sync.dma_start(
-            out=grad_rows[:].rearrange("p (b e) n -> p b (e n)", b=BATCH), in_=grad_view
-        )
+        load_tokens(grad_rows, grad_view)
         attn_rows = []
         for c in range(CLUSTERS):
             rows = rows_pool.tile([P, PACK, G], BF16, name="rows")
-            nc.sync.dma_start(
-                out=rows[:].rearrange("p (b e) g -> p b (e g)", b=BATCH), in_=attn_view[:, :, c, :]
-            )
+            load_tokens(rows, attn_view[:, c])
             attn_rows.append(rows)
 
         probs = const.tile([P, CLUSTERS, PACK], BF16)
-        nc.vector.tensor_copy(out=probs[:], in_=probs_rows[:].rearrange("p t c -> p c t"))
+        nc.scalar.copy(out=probs[:], in_=probs_rows[:].rearrange("p t c -> p c t"))
         grad = const.tile([P, E, PACK], BF16)
-        regroup(
-            nc,
-            grad[:].rearrange("p (r i) t -> p r t i", i=RUN),
-            grad_rows[:].rearrange("p t (r i) -> p r t i", i=RUN),
+        nc.vector.tensor_copy(
+            out=grad[:].rearrange("p (r i) t -> p r t i", i=RUN),
+            in_=grad_rows[:].rearrange("p t (r i) -> p r t i", i=RUN),
         )
 
         def quantise_cluster(c):
@@ -101,6 +99,7 @@ def tile_model_pa_kernel(tc, attn_ctx, Wo, bo, cluster_probs, grad_out, out):
 
         def multiply_cluster(c, operands):
             attn_codes, attn_scales, gp_codes, gp_scales = operands
+            last = c == CLUSTERS - 1
             result = result_pool.tile([P, M_TILES, E], F32)
             for i in range(M_TILES):
                 m_cols = slice(i * M_TILE, (i + 1) * M_TILE)
@@ -114,11 +113,17 @@ def tile_model_pa_kernel(tc, attn_ctx, Wo, bo, cluster_probs, grad_out, out):
                     start=True,
                     stop=True,
                 )
-                nc.scalar.copy(out=result[:, i, :], in_=acc[:])
-            nc.sync.dma_start(out=out_view[c], in_=result[:].rearrange("p i e -> p (i e)"))
+                if last and i % 2 == 1:
+                    nc.vector.tensor_copy(out=result[:, i, :], in_=acc[:])
+                else:
+                    nc.scalar.copy(out=result[:, i, :], in_=acc[:])
+                if last:
+                    nc.sync.dma_start(out=out_view[c][:, i, :], in_=result[:, i, :])
+            if not last:
+                nc.sync.dma_start(out=out_view[c], in_=result[:])
 
-        operands = quantise_cluster(0)
+        operands = [quantise_cluster(c) for c in range(AHEAD)]
         for c in range(CLUSTERS):
-            following = quantise_cluster(c + 1) if c + 1 < CLUSTERS else None
-            multiply_cluster(c, operands)
-            operands = following
+            if c + AHEAD < CLUSTERS:
+                operands.append(quantise_cluster(c + AHEAD))
+            multiply_cluster(c, operands[c])

@@ -1,4 +1,5 @@
 import concourse.mybir as mybir
+from concourse.masks import make_identity
 
 F32 = mybir.dt.float32
 BF16 = mybir.dt.bfloat16
@@ -18,7 +19,9 @@ M_TILES = G // M_TILE
 
 RUN = 4
 RUNS = G // RUN
-VECTOR_RUNS = RUNS * 5 // 8
+VECTOR_RUNS = RUNS // 2
+TENSOR_RUNS = RUNS * 3 // 8
+SCALAR_END = RUNS - TENSOR_RUNS
 assert RUN == M_TILES
 
 AHEAD = 2
@@ -29,7 +32,7 @@ BYTES = 2 * CLUSTERS * G * P * PACK + 2 * CLUSTERS * P * PACK + 2 * E * P * PACK
 
 def regroup(nc, grouped, rows):
     nc.vector.tensor_copy(out=grouped[:, :VECTOR_RUNS], in_=rows[:, :VECTOR_RUNS])
-    nc.scalar.copy(out=grouped[:, VECTOR_RUNS:], in_=rows[:, VECTOR_RUNS:])
+    nc.scalar.copy(out=grouped[:, VECTOR_RUNS:SCALAR_END], in_=rows[:, VECTOR_RUNS:SCALAR_END])
 
 
 def tile_model_pa_kernel(tc, attn_ctx, Wo, bo, cluster_probs, grad_out, out):
@@ -44,10 +47,13 @@ def tile_model_pa_kernel(tc, attn_ctx, Wo, bo, cluster_probs, grad_out, out):
         name="rows", bufs=CLUSTERS
     ) as rows_pool, tc.tile_pool(name="work", bufs=AHEAD + 2) as work, tc.tile_pool(
         name="result", bufs=8
-    ) as result_pool, tc.psum_pool(name="psum", bufs=8) as psum, tc.manual_schedule():
+    ) as result_pool, tc.psum_pool(name="psum", bufs=6) as psum, tc.psum_pool(name="mixed", bufs=2) as mixed_pool, tc.manual_schedule():
         def load_tokens(rows, view):
             for b in range(BATCH):
                 nc.sync.dma_start(out=rows[b:P:BATCH].rearrange("p t w -> p (t w)"), in_=view[b])
+
+        identity = const.tile([P, P], BF16)
+        make_identity(nc, identity[:])
 
         probs_rows = const.tile([P, PACK, CLUSTERS], BF16)
         load_tokens(probs_rows, probs_view)
@@ -73,6 +79,20 @@ def tile_model_pa_kernel(tc, attn_ctx, Wo, bo, cluster_probs, grad_out, out):
                 nc,
                 attn[:].rearrange("p (i m) t -> p m t i", i=M_TILES),
                 attn_rows[c][:].rearrange("p t (m i) -> p m t i", i=M_TILES),
+            )
+            mixed = mixed_pool.tile([P, M_TILES, TENSOR_RUNS, PACK], BF16)
+            moving = attn_rows[c][:].rearrange("p t (m i) -> p i m t", i=M_TILES)
+            for half in range(2):
+                tiles = slice(half * M_TILES // 2, (half + 1) * M_TILES // 2)
+                nc.tensor.matmul(
+                    out=mixed[:, tiles],
+                    lhsT=identity[:],
+                    rhs=moving[:, tiles, SCALAR_END:, :],
+                    start=True,
+                    stop=True,
+                )
+            nc.scalar.copy(
+                out=attn[:].rearrange("p (i m) t -> p i m t", i=M_TILES)[:, :, SCALAR_END:, :], in_=mixed[:]
             )
             gp = work.tile([P, E, PACK], BF16, align_bytes=64)
             nc.vector.tensor_tensor(

import concourse.mybir as mybir
from concourse.masks import make_identity

F32 = mybir.dt.float32
BF16 = mybir.dt.bfloat16
U32 = mybir.dt.uint32
U8 = mybir.dt.uint8
E4M3_X4 = mybir.dt.float8_e4m3fn_x4
E5M2_X4 = mybir.dt.float8_e5m2_x4

P = 128
PACK = 4
BATCH = 2
CLUSTERS = 16
G = 512
E = 512
M_TILE = 128
M_TILES = G // M_TILE

RUN = 4
RUNS = G // RUN
VECTOR_RUNS = RUNS // 2
TENSOR_RUNS = RUNS * 3 // 8
SCALAR_END = RUNS - TENSOR_RUNS
assert RUN == M_TILES

AHEAD = 2

FLOPS = 2 * CLUSTERS * G * E * P * PACK
BYTES = 2 * CLUSTERS * G * P * PACK + 2 * CLUSTERS * P * PACK + 2 * E * P * PACK + 4 * CLUSTERS * G * E


def regroup(nc, grouped, rows):
    nc.vector.tensor_copy(out=grouped[:, :VECTOR_RUNS], in_=rows[:, :VECTOR_RUNS])
    nc.scalar.copy(out=grouped[:, VECTOR_RUNS:SCALAR_END], in_=rows[:, VECTOR_RUNS:SCALAR_END])


def tile_model_pa_kernel(tc, attn_ctx, Wo, bo, cluster_probs, grad_out, out):
    nc = tc.nc

    attn_view = attn_ctx.rearrange("b c (q t) h d -> b c q (t h d)", t=PACK)
    probs_view = cluster_probs.rearrange("b (q t) c -> b q (t c)", t=PACK)
    grad_view = grad_out.rearrange("b (q t) n -> b q (t n)", t=PACK)
    out_view = out.rearrange("c h d e -> c (h d) e").rearrange("c (m i) e -> c m i e", i=M_TILES)

    with tc.tile_pool(name="const", bufs=1) as const, tc.tile_pool(
        name="rows", bufs=CLUSTERS
    ) as rows_pool, tc.tile_pool(name="work", bufs=AHEAD + 2) as work, tc.tile_pool(
        name="result", bufs=8
    ) as result_pool, tc.psum_pool(name="psum", bufs=6) as psum, tc.psum_pool(name="mixed", bufs=2) as mixed_pool, tc.manual_schedule():
        def load_tokens(rows, view):
            for b in range(BATCH):
                nc.sync.dma_start(out=rows[b:P:BATCH].rearrange("p t w -> p (t w)"), in_=view[b])

        identity = const.tile([P, P], BF16)
        make_identity(nc, identity[:])

        probs_rows = const.tile([P, PACK, CLUSTERS], BF16)
        load_tokens(probs_rows, probs_view)
        grad_rows = const.tile([P, PACK, E], BF16)
        load_tokens(grad_rows, grad_view)
        attn_rows = []
        for c in range(CLUSTERS):
            rows = rows_pool.tile([P, PACK, G], BF16, name="rows")
            load_tokens(rows, attn_view[:, c])
            attn_rows.append(rows)

        probs = const.tile([P, CLUSTERS, PACK], BF16)
        nc.scalar.copy(out=probs[:], in_=probs_rows[:].rearrange("p t c -> p c t"))
        grad = const.tile([P, E, PACK], BF16)
        nc.vector.tensor_copy(
            out=grad[:].rearrange("p (r i) t -> p r t i", i=RUN),
            in_=grad_rows[:].rearrange("p t (r i) -> p r t i", i=RUN),
        )

        def quantise_cluster(c):
            attn = work.tile([P, G, PACK], BF16, align_bytes=64)
            regroup(
                nc,
                attn[:].rearrange("p (i m) t -> p m t i", i=M_TILES),
                attn_rows[c][:].rearrange("p t (m i) -> p m t i", i=M_TILES),
            )
            mixed = mixed_pool.tile([P, M_TILES, TENSOR_RUNS, PACK], BF16)
            moving = attn_rows[c][:].rearrange("p t (m i) -> p i m t", i=M_TILES)
            for half in range(2):
                tiles = slice(half * M_TILES // 2, (half + 1) * M_TILES // 2)
                nc.tensor.matmul(
                    out=mixed[:, tiles],
                    lhsT=identity[:],
                    rhs=moving[:, tiles, SCALAR_END:, :],
                    start=True,
                    stop=True,
                )
            nc.scalar.copy(
                out=attn[:].rearrange("p (i m) t -> p i m t", i=M_TILES)[:, :, SCALAR_END:, :], in_=mixed[:]
            )
            gp = work.tile([P, E, PACK], BF16, align_bytes=64)
            nc.vector.tensor_tensor(
                out=gp[:],
                in0=grad[:],
                in1=probs[:, c, :].unsqueeze(1).to_broadcast([P, E, PACK]),
                op=mybir.AluOpType.mult,
            )
            attn_codes = work.tile([P, G], U32, align_bytes=64)
            attn_scales = work.tile([P, G], U8, align_bytes=64)
            nc.vector.quantize_mx(
                out=attn_codes[:].bitcast(E4M3_X4),
                scales=attn_scales[:],
                in_=attn[:].rearrange("p w t -> p (w t)"),
            )
            gp_codes = work.tile([P, E], U32, align_bytes=64)
            gp_scales = work.tile([P, E], U8, align_bytes=64)
            nc.vector.quantize_mx(
                out=gp_codes[:].bitcast(E5M2_X4),
                scales=gp_scales[:],
                in_=gp[:].rearrange("p w t -> p (w t)"),
            )
            return attn_codes, attn_scales, gp_codes, gp_scales

        def multiply_cluster(c, operands):
            attn_codes, attn_scales, gp_codes, gp_scales = operands
            last = c == CLUSTERS - 1
            result = result_pool.tile([P, M_TILES, E], F32)
            for i in range(M_TILES):
                m_cols = slice(i * M_TILE, (i + 1) * M_TILE)
                acc = psum.tile([M_TILE, E], F32)
                nc.tensor.matmul_mx(
                    out=acc[:],
                    lhsT=attn_codes[:, m_cols].bitcast(E4M3_X4),
                    lhsT_scale=attn_scales[:, m_cols],
                    rhs=gp_codes[:].bitcast(E5M2_X4),
                    rhs_scale=gp_scales[:],
                    start=True,
                    stop=True,
                )
                if last and i % 2 == 1:
                    nc.vector.tensor_copy(out=result[:, i, :], in_=acc[:])
                else:
                    nc.scalar.copy(out=result[:, i, :], in_=acc[:])
                if last:
                    nc.sync.dma_start(out=out_view[c][:, i, :], in_=result[:, i, :])
            if not last:
                nc.sync.dma_start(out=out_view[c], in_=result[:])

        operands = [quantise_cluster(c) for c in range(AHEAD)]
        for c in range(CLUSTERS):
            if c + AHEAD < CLUSTERS:
                operands.append(quantise_cluster(c + AHEAD))
            multiply_cluster(c, operands[c])
